import numpy as np
import ml_dtypes


def mxq(x, axis, fmt="e4m3"):
    dtype, down = {"e4m3": (ml_dtypes.float8_e4m3fn, 7), "e5m2": (ml_dtypes.float8_e5m2, 14)}[fmt]
    v = np.moveaxis(np.asarray(x, np.float32).astype(ml_dtypes.bfloat16).astype(np.float64), axis, -1)
    blocks = v.reshape(v.shape[:-1] + (-1, 32))
    amax = np.abs(blocks).max(-1, keepdims=True)
    byte = np.maximum(np.where(amax > 0, np.frexp(amax)[1] - 1 + 127, 0) - down, 1)
    scale = np.exp2(byte - 127.0)
    codes = (blocks / scale).astype(np.float32).astype(dtype).astype(np.float64)
    return np.moveaxis((codes * scale).reshape(v.shape), -1, axis)


WIDE = False


def mx_kscale(k):
    if not WIDE:
        return np.ones(k)
    levels = np.array([10, -10, 5, -5, 0])
    a = np.random.permutation(np.resize(levels, k // 512 * 4)).reshape(k // 512, 4)
    idx = np.arange(k)
    return np.exp2(a[idx // 512, idx % 128 // 32])


BF16 = ml_dtypes.bfloat16


def bf(x):
    return np.asarray(x, np.float32).astype(BF16)


def f64(x):
    return np.asarray(x).astype(np.float64)


E2M1 = np.array([0.0, 0.5, 1.0, 1.5, 2.0, 3.0, 4.0, 6.0, -0.0, -0.5, -1.0, -1.5, -2.0, -3.0, -4.0, -6.0])


def pack_weight(w, fmt):
    k, n = w.shape
    w = f64(bf(w)).reshape(k // 32, 32, n)
    amax = np.abs(w).max(1)
    if fmt == "e4m3":
        byte = np.frexp(amax)[1] - 1 + 127 - 7
    else:
        mant, ex = np.frexp(amax / 6.0)
        byte = np.where(mant > 0.5, ex, ex - 1) + 127
    byte = np.clip(np.where(amax > 0, byte, 1), 1, 254)
    scaled = (w * np.exp2(127.0 - byte)[:, None, :]).reshape(k, n).astype(np.float32)
    by_word = np.ascontiguousarray(scaled.reshape(k // 512, 128, 4, n).transpose(0, 1, 3, 2))
    if fmt == "e4m3":
        words = by_word.astype(ml_dtypes.float8_e4m3fn).view(np.uint8)
    else:
        c = by_word.astype(ml_dtypes.float4_e2m1fn).view(np.uint8) & 0xF
        words = c[..., 0::2] | (c[..., 1::2] << 4)
    return np.ascontiguousarray(words), np.ascontiguousarray(byte.astype(np.uint8).reshape(k // 512, 16, n))


def unpack_weight(words, scales, fmt):
    g, p, n, _ = words.shape
    if fmt == "e4m3":
        vals = np.ascontiguousarray(words).view(ml_dtypes.float8_e4m3fn).astype(np.float64)
    else:
        nib = np.empty((g, p, n, 4), np.uint8)
        nib[..., 0::2] = words & 0xF
        nib[..., 1::2] = words >> 4
        vals = E2M1[nib]
    vals = vals * np.repeat(np.exp2(scales.astype(np.float64) - 127.0), 8, axis=1)[..., None]
    return vals.transpose(0, 1, 3, 2).reshape(g * 512, n)

def pack4(w):
    words, scales = pack_weight(w, "e2m1")
    return words.reshape(words.shape[0], 128, -1), scales


def unpack4(words, scales):
    return unpack_weight(words.reshape(words.shape[0], 128, -1, 2), scales, "e2m1")


B, N, D, H, DH = 2, 512, 1024, 16, 64
INNER = H * DH


def dpfp(u):
    u2 = np.concatenate([np.maximum(u, 0.0), np.maximum(-u, 0.0)], axis=-1)
    return u2 * np.roll(u2, 1, axis=-1)


def heads(t):
    return t.reshape(B, N, H, DH).transpose(0, 2, 1, 3)


def setup_inputs():
    s = mx_kscale(D)
    x = bf(np.random.standard_normal((B, N, D)) * s)
    words, scales = pack4(np.random.standard_normal((D, 2 * INNER)) / np.sqrt(D) / s[:, None])
    return {"x": x, "w_qk_words": words, "w_qk_scales": scales}


def reference(x, w_qk_words, w_qk_scales):
    qk = mxq(f64(x), 2, "e4m3") @ unpack4(w_qk_words, w_qk_scales)
    q, k = np.split(qk, 2, axis=-1)
    q, k = dpfp(heads(q)), dpfp(heads(k))
    return q / q.sum(-1, keepdims=True), k / k.sum(-1, keepdims=True)

@@ -1,0 +1,201 @@
+from contextlib import ExitStack
+
+import concourse.mybir as mybir
+from concourse.masks import make_identity
+
+F32 = mybir.dt.float32
+BF16 = mybir.dt.bfloat16
+I32 = mybir.dt.int32
+U32 = mybir.dt.uint32
+U8 = mybir.dt.uint8
+FP8X4 = mybir.dt.float8_e4m3fn_x4
+FP4X4 = mybir.dt.float4_e2m1fn_x4
+ALU = mybir.AluOpType
+ACT = mybir.ActivationFunctionType
+
+P = 128
+PACK = 4
+BATCH, TOKENS, D_MODEL = 2, 512, 1024
+HEADS, D_HEAD = 16, 64
+COLS = 2 * HEADS * D_HEAD
+PASSES = D_MODEL // (P * PACK)
+SUBTILES = TOKENS // P
+BANK_COLS = 512
+BANKS = COLS // BANK_COLS
+BANK_HEADS = BANK_COLS // D_HEAD
+PAD = 4
+
+FLOPS = 2 * BATCH * TOKENS * D_MODEL * COLS
+
+
+def tile_dpfpattention_pa_kernel(tc, x, w_qk_words, w_qk_scales, out_0, out_1):
+    nc = tc.nc
+    outs = (out_0, out_1)
+    with ExitStack() as ctx:
+        keep = ctx.enter_context(tc.tile_pool(name="keep", bufs=1))
+        stage = ctx.enter_context(tc.tile_pool(name="stage", bufs=2))
+        work = ctx.enter_context(tc.tile_pool(name="work", bufs=4))
+        results = ctx.enter_context(tc.tile_pool(name="results", bufs=3))
+        psum_x = ctx.enter_context(tc.psum_pool(name="psum_x", bufs=2))
+        psum_u = ctx.enter_context(tc.psum_pool(name="psum_u", bufs=6))
+
+        identity = keep.tile([P, P], F32)
+        make_identity(nc, identity[:])
+
+        x_sb = keep.tile([P, BATCH, SUBTILES, D_MODEL], BF16)
+        w_words = keep.tile([P, PASSES, 2 * COLS], U8, align_bytes=64)
+        w_scales = keep.tile([P, PASSES, COLS], U8, align_bytes=64)
+        x_codes = keep.tile([P, BATCH * SUBTILES, PASSES * P], U32, align_bytes=64)
+        x_scales = keep.tile([P, BATCH * SUBTILES, PASSES * P], U8, align_bytes=64)
+
+        nc.vector.memset(w_scales[:].bitcast(I32), 0)
+        x_rows = x.rearrange("b (p j) k -> b p j k", j=SUBTILES)
+        words_i32 = w_qk_words.bitcast(I32).rearrange("g p c -> p g c")
+        scales_i32 = w_qk_scales.bitcast(I32).rearrange("g q c -> q g c")
+        plane_i32 = w_scales[:].bitcast(I32)
+
+        def load_x(b, j):
+            nc.sync.dma_start(out=x_sb[:, b, j, :], in_=x_rows[b, :, j, :])
+
+        def load_w(n):
+            nc.sync.dma_start(
+                out=w_words[:, :, 2 * BANK_COLS * n : 2 * BANK_COLS * (n + 1)].bitcast(I32),
+                in_=words_i32[:, :, BANK_COLS // 2 * n : BANK_COLS // 2 * (n + 1)],
+            )
+
+        load_x(0, 0)
+        for r in range(4):
+            nc.sync.dma_start(out=plane_i32[r:P:32, :, :], in_=scales_i32[r:16:4, :, :])
+        load_w(0)
+        for j in range(1, SUBTILES):
+            load_x(0, j)
+        for n in range(1, BANKS):
+            load_w(n)
+        nc.sync.dma_start(out=x_sb[:, 1, :, :], in_=x_rows[1])
+
+        def quantise_x(b, j):
+            x_pairs = x_sb[:, b, j, :].bitcast(F32)
+            turned = psum_x.tile([P, PASSES, 2, P], F32)
+            for g in range(PASSES):
+                for e in range(2):
+                    nc.tensor.transpose(
+                        turned[:, g, e, :],
+                        x_pairs[:, 2 * P * g + e : 2 * P * (g + 1) : 2],
+                        identity[:],
+                    )
+            grouped = stage.tile([P, PASSES * P * PACK], BF16, align_bytes=64)
+            nc.scalar.copy(
+                out=grouped[:].bitcast(F32).rearrange("p (g r e) -> p g r e", g=PASSES, e=2),
+                in_=turned[:].rearrange("p g e r -> p g r e"),
+            )
+            nc.vector.quantize_mx(
+                out=x_codes[:, SUBTILES * b + j, :].bitcast(FP8X4),
+                scales=x_scales[:, SUBTILES * b + j, :],
+                in_=grouped[:],
+            )
+
+        units = [(b, n, j) for b in range(BATCH) for n in range(BANKS) for j in range(SUBTILES)]
+        live = {}
+
+        def project(i):
+            b, n, j = units[i]
+            u = psum_u.tile([P, BANK_COLS], F32)
+            for g in range(PASSES):
+                nc.tensor.matmul_mx(
+                    out=u[:],
+                    lhsT=x_codes[:, SUBTILES * b + j, P * g : P * (g + 1)].bitcast(FP8X4),
+                    lhsT_scale=x_scales[:, SUBTILES * b + j, P * g : P * (g + 1)],
+                    rhs=w_words[:, g, 2 * BANK_COLS * n : 2 * BANK_COLS * (n + 1)].bitcast(FP4X4),
+                    rhs_scale=w_scales[:, g, BANK_COLS * n : BANK_COLS * (n + 1)],
+                    start=(g == 0),
+                    stop=(g == PASSES - 1),
+                )
+            before = work.tile([P, PAD + BANK_COLS], F32)
+            nc.scalar.copy(out=before[:, PAD:], in_=u[:])
+            nc.scalar.mul(
+                out=before[:, PAD - 1 : PAD - 1 + BANK_COLS : D_HEAD],
+                in_=u[:, D_HEAD - 1 : BANK_COLS : D_HEAD],
+                mul=-1.0,
+            )
+            live["u", i] = u
+            live["before", i] = before
+
+        def pair_products(i):
+            pair = work.tile([P, BANK_COLS], F32)
+            nc.vector.tensor_tensor(
+                out=pair[:],
+                in0=live["u", i][:],
+                in1=live["before", i][:, PAD - 1 : PAD - 1 + BANK_COLS],
+                op=ALU.mult,
+            )
+            live["pair", i] = pair
+
+        def normalise(i):
+            pair = live["pair", i]
+            kept = work.tile([P, BANK_HEADS, D_HEAD], F32)
+            total = work.tile([P, BANK_HEADS], F32)
+            for h in range(BANK_HEADS):
+                nc.scalar.activation(
+                    out=kept[:, h, :],
+                    in_=pair[:, D_HEAD * h : D_HEAD * (h + 1)],
+                    func=ACT.Relu,
+                    accum_out=total[:, h : h + 1],
+                )
+            inverse = work.tile([P, BANK_HEADS], F32)
+            nc.vector.reciprocal(out=inverse[:], in_=total[:])
+            share = work.tile([P, BANK_HEADS, D_HEAD], F32)
+            nc.gpsimd.tensor_tensor(
+                out=share[:],
+                in0=kept[:],
+                in1=inverse[:].unsqueeze(2).to_broadcast([P, BANK_HEADS, D_HEAD]),
+                op=ALU.mult,
+            )
+            live["share", i] = share
+
+        def split_by_sign(i):
+            b, n, j = units[i]
+            if j == 0:
+                result = results.tile([P, BANK_HEADS, SUBTILES, 2 * D_HEAD], F32)
+                live["result", b, n] = result
+            result = live["result", b, n]
+            u_heads = live["u", i][:].rearrange("p (h c) -> p h c", c=D_HEAD)
+            nc.vector.scalar_tensor_tensor(
+                out=result[:, :, j, 0:D_HEAD],
+                in0=u_heads,
+                scalar=0.0,
+                in1=live["share", i][:],
+                op0=ALU.is_gt,
+                op1=ALU.mult,
+            )
+            nc.vector.scalar_tensor_tensor(
+                out=result[:, :, j, D_HEAD : 2 * D_HEAD],
+                in0=u_heads,
+                scalar=0.0,
+                in1=live["share", i][:],
+                op0=ALU.is_lt,
+                op1=ALU.mult,
+            )
+            if j == SUBTILES - 1:
+                first_head = BANK_HEADS * (n % 2)
+                nc.sync.dma_start(
+                    out=outs[n // 2][b, first_head : first_head + BANK_HEADS].rearrange(
+                        "h (p j) f -> p h (j f)", j=SUBTILES
+                    ),
+                    in_=result[:].rearrange("p h j f -> p h (j f)"),
+                )
+
+        for j in range(SUBTILES):
+            quantise_x(0, j)
+        project(0)
+        for i in range(len(units) + 2):
+            if i + 1 < len(units):
+                project(i + 1)
+            if i < len(units):
+                pair_products(i)
+            if i >= 2:
+                split_by_sign(i - 2)
+            if i < len(units):
+                normalise(i)
+            if i == SUBTILES:
+                for j in range(SUBTILES):
+                    quantise_x(1, j)

@@ -21,9 +21,11 @@ COLS = 2 * HEADS * D_HEAD
 PASSES = D_MODEL // (P * PACK)
 SUBTILES = TOKENS // P
 BANK_COLS = 512
-BANKS = COLS // BANK_COLS
-BANK_HEADS = BANK_COLS // D_HEAD
+RANGES = COLS // BANK_COLS
+RANGE_HEADS = BANK_COLS // D_HEAD
 PAD = 4
+SCALE_ROWS = P * PACK // 32
+LAG = 3
 
 FLOPS = 2 * BATCH * TOKENS * D_MODEL * COLS
 
@@ -32,6 +34,7 @@ def tile_dpfpattention_pa_kernel(tc, x, w_qk_words, w_qk_scales, out_0, out_1):
     nc = tc.nc
     outs = (out_0, out_1)
     with ExitStack() as ctx:
+        ctx.enter_context(tc.manual_schedule())
         keep = ctx.enter_context(tc.tile_pool(name="keep", bufs=1))
         stage = ctx.enter_context(tc.tile_pool(name="stage", bufs=2))
         work = ctx.enter_context(tc.tile_pool(name="work", bufs=4))
@@ -65,15 +68,17 @@ def tile_dpfpattention_pa_kernel(tc, x, w_qk_words, w_qk_scales, out_0, out_1):
 
         load_x(0, 0)
         for r in range(4):
-            nc.sync.dma_start(out=plane_i32[r:P:32, :, :], in_=scales_i32[r:16:4, :, :])
+            nc.sync.dma_start(out=plane_i32[r:P:32, :, :], in_=scales_i32[r:SCALE_ROWS:4, :, :])
         load_w(0)
         for j in range(1, SUBTILES):
             load_x(0, j)
-        for n in range(1, BANKS):
+        for n in range(1, RANGES):
             load_w(n)
         nc.sync.dma_start(out=x_sb[:, 1, :, :], in_=x_rows[1])
 
-        def quantise_x(b, j):
+        live = {}
+
+        def turn_x(b, j, copy):
             x_pairs = x_sb[:, b, j, :].bitcast(F32)
             turned = psum_x.tile([P, PASSES, 2, P], F32)
             for g in range(PASSES):
@@ -84,18 +89,21 @@ def tile_dpfpattention_pa_kernel(tc, x, w_qk_words, w_qk_scales, out_0, out_1):
                         identity[:],
                     )
             grouped = stage.tile([P, PASSES * P * PACK], BF16, align_bytes=64)
-            nc.scalar.copy(
+            copy(
                 out=grouped[:].bitcast(F32).rearrange("p (g r e) -> p g r e", g=PASSES, e=2),
                 in_=turned[:].rearrange("p g e r -> p g r e"),
             )
+            live["grouped", b, j] = grouped
+
+        def quantise_x(b, j):
             nc.vector.quantize_mx(
                 out=x_codes[:, SUBTILES * b + j, :].bitcast(FP8X4),
                 scales=x_scales[:, SUBTILES * b + j, :],
-                in_=grouped[:],
+                in_=live["grouped", b, j][:],
             )
 
-        units = [(b, n, j) for b in range(BATCH) for n in range(BANKS) for j in range(SUBTILES)]
-        live = {}
+        units = [(b, n, j) for b in range(BATCH) for n in range(RANGES) for j in range(SUBTILES)]
+        n_units = len(units)
 
         def project(i):
             b, n, j = units[i]
@@ -110,44 +118,49 @@ def tile_dpfpattention_pa_kernel(tc, x, w_qk_words, w_qk_scales, out_0, out_1):
                     start=(g == 0),
                     stop=(g == PASSES - 1),
                 )
-            before = work.tile([P, PAD + BANK_COLS], F32)
-            nc.scalar.copy(out=before[:, PAD:], in_=u[:])
+            live["u", i] = u
+
+        def neighbours(i):
+            u = live["u", i]
+            shifted = work.tile([P, PAD + BANK_COLS], F32)
+            nc.scalar.copy(out=shifted[:, PAD:], in_=u[:])
+            before = shifted[:, PAD - 1 : PAD - 1 + BANK_COLS]
             nc.scalar.mul(
-                out=before[:, PAD - 1 : PAD - 1 + BANK_COLS : D_HEAD],
+                out=before[:, 0:BANK_COLS:D_HEAD],
                 in_=u[:, D_HEAD - 1 : BANK_COLS : D_HEAD],
                 mul=-1.0,
             )
-            live["u", i] = u
             live["before", i] = before
 
         def pair_products(i):
             pair = work.tile([P, BANK_COLS], F32)
             nc.vector.tensor_tensor(
-                out=pair[:],
-                in0=live["u", i][:],
-                in1=live["before", i][:, PAD - 1 : PAD - 1 + BANK_COLS],
-                op=ALU.mult,
+                out=pair[:], in0=live["u", i][:], in1=live["before", i], op=ALU.mult
             )
             live["pair", i] = pair
 
-        def normalise(i):
+        def sums(i):
             pair = live["pair", i]
-            kept = work.tile([P, BANK_HEADS, D_HEAD], F32)
-            total = work.tile([P, BANK_HEADS], F32)
-            for h in range(BANK_HEADS):
+            kept = work.tile([P, RANGE_HEADS, D_HEAD], F32)
+            total = work.tile([P, RANGE_HEADS], F32)
+            for h in range(RANGE_HEADS):
                 nc.scalar.activation(
                     out=kept[:, h, :],
                     in_=pair[:, D_HEAD * h : D_HEAD * (h + 1)],
                     func=ACT.Relu,
                     accum_out=total[:, h : h + 1],
                 )
-            inverse = work.tile([P, BANK_HEADS], F32)
-            nc.vector.reciprocal(out=inverse[:], in_=total[:])
-            share = work.tile([P, BANK_HEADS, D_HEAD], F32)
+            live["kept", i] = kept
+            live["total", i] = total
+
+        def shares(i):
+            inverse = work.tile([P, RANGE_HEADS], F32)
+            nc.vector.reciprocal(out=inverse[:], in_=live["total", i][:])
+            share = work.tile([P, RANGE_HEADS, D_HEAD], F32)
             nc.gpsimd.tensor_tensor(
                 out=share[:],
-                in0=kept[:],
-                in1=inverse[:].unsqueeze(2).to_broadcast([P, BANK_HEADS, D_HEAD]),
+                in0=live["kept", i][:],
+                in1=inverse[:].unsqueeze(2).to_broadcast([P, RANGE_HEADS, D_HEAD]),
                 op=ALU.mult,
             )
             live["share", i] = share
@@ -155,47 +168,55 @@ def tile_dpfpattention_pa_kernel(tc, x, w_qk_words, w_qk_scales, out_0, out_1):
         def split_by_sign(i):
             b, n, j = units[i]
             if j == 0:
-                result = results.tile([P, BANK_HEADS, SUBTILES, 2 * D_HEAD], F32)
+                result = results.tile([P, RANGE_HEADS, SUBTILES, 2 * D_HEAD], F32)
                 live["result", b, n] = result
             result = live["result", b, n]
             u_heads = live["u", i][:].rearrange("p (h c) -> p h c", c=D_HEAD)
-            nc.vector.scalar_tensor_tensor(
-                out=result[:, :, j, 0:D_HEAD],
-                in0=u_heads,
-                scalar=0.0,
-                in1=live["share", i][:],
-                op0=ALU.is_gt,
-                op1=ALU.mult,
+            for half, sign_test in enumerate((ALU.is_gt, ALU.is_lt)):
+                nc.vector.scalar_tensor_tensor(
+                    out=result[:, :, j, D_HEAD * half : D_HEAD * (half + 1)],
+                    in0=u_heads,
+                    scalar=0.0,
+                    in1=live["share", i][:],
+                    op0=sign_test,
+                    op1=ALU.mult,
+                )
+            first_head = RANGE_HEADS * (n % 2)
+            rows = outs[n // 2][b, first_head : first_head + RANGE_HEADS].rearrange(
+                "h (p j) f -> p h j f", j=SUBTILES
             )
-            nc.vector.scalar_tensor_tensor(
-                out=result[:, :, j, D_HEAD : 2 * D_HEAD],
-                in0=u_heads,
-                scalar=0.0,
-                in1=live["share", i][:],
-                op0=ALU.is_lt,
-                op1=ALU.mult,
-            )
-            if j == SUBTILES - 1:
-                first_head = BANK_HEADS * (n % 2)
+            if i >= n_units - SUBTILES:
+                nc.sync.dma_start(out=rows[:, :, j, :], in_=result[:, :, j, :])
+            elif j == SUBTILES - 1:
                 nc.sync.dma_start(
-                    out=outs[n // 2][b, first_head : first_head + BANK_HEADS].rearrange(
-                        "h (p j) f -> p h (j f)", j=SUBTILES
-                    ),
+                    out=rows.rearrange("p h j f -> p h (j f)"),
                     in_=result[:].rearrange("p h j f -> p h (j f)"),
                 )
 
-        for j in range(SUBTILES):
+        def prepare_x0(j):
+            turn_x(0, j, nc.vector.tensor_copy)
             quantise_x(0, j)
+
+        prepare_x0(0)
+        prepare_x0(1)
         project(0)
-        for i in range(len(units) + 2):
-            if i + 1 < len(units):
-                project(i + 1)
-            if i < len(units):
+        neighbours(0)
+        for i in range(n_units + LAG):
+            turn_next = i < n_units and units[i][0] == 0 and units[i][2] == SUBTILES - 1
+            if i < n_units:
                 pair_products(i)
-            if i >= 2:
-                split_by_sign(i - 2)
-            if i < len(units):
-                normalise(i)
-            if i == SUBTILES:
-                for j in range(SUBTILES):
-                    quantise_x(1, j)
+            if 1 <= i <= n_units:
+                shares(i - 1)
+            if i + 2 < SUBTILES:
+                prepare_x0(i + 2)
+            if i + 1 < n_units:
+                project(i + 1)
+                neighbours(i + 1)
+            if turn_next:
+                turn_x(1, units[i][1], nc.scalar.copy)
+            if i >= LAG:
+                split_by_sign(i - LAG)
+            if turn_next:
+                quantise_x(1, units[i][1])
+            if i < n_units:
+                sums(i)

@@ -25,7 +25,7 @@ RANGES = COLS // BANK_COLS
 RANGE_HEADS = BANK_COLS // D_HEAD
 PAD = 4
 SCALE_ROWS = P * PACK // 32
-LAG = 3
+LAG = 2
 
 FLOPS = 2 * BATCH * TOKENS * D_MODEL * COLS
 
@@ -34,7 +34,6 @@ def tile_dpfpattention_pa_kernel(tc, x, w_qk_words, w_qk_scales, out_0, out_1):
     nc = tc.nc
     outs = (out_0, out_1)
     with ExitStack() as ctx:
-        ctx.enter_context(tc.manual_schedule())
         keep = ctx.enter_context(tc.tile_pool(name="keep", bufs=1))
         stage = ctx.enter_context(tc.tile_pool(name="stage", bufs=2))
         work = ctx.enter_context(tc.tile_pool(name="work", bufs=4))
@@ -78,7 +77,7 @@ def tile_dpfpattention_pa_kernel(tc, x, w_qk_words, w_qk_scales, out_0, out_1):
 
         live = {}
 
-        def turn_x(b, j, copy):
+        def turn_x(b, j):
             x_pairs = x_sb[:, b, j, :].bitcast(F32)
             turned = psum_x.tile([P, PASSES, 2, P], F32)
             for g in range(PASSES):
@@ -89,7 +88,7 @@ def tile_dpfpattention_pa_kernel(tc, x, w_qk_words, w_qk_scales, out_0, out_1):
                         identity[:],
                     )
             grouped = stage.tile([P, PASSES * P * PACK], BF16, align_bytes=64)
-            copy(
+            nc.scalar.copy(
                 out=grouped[:].bitcast(F32).rearrange("p (g r e) -> p g r e", g=PASSES, e=2),
                 in_=turned[:].rearrange("p g e r -> p g r e"),
             )
@@ -193,30 +192,23 @@ def tile_dpfpattention_pa_kernel(tc, x, w_qk_words, w_qk_scales, out_0, out_1):
                     in_=result[:].rearrange("p h j f -> p h (j f)"),
                 )
 
-        def prepare_x0(j):
-            turn_x(0, j, nc.vector.tensor_copy)
+        for j in range(SUBTILES):
+            turn_x(0, j)
             quantise_x(0, j)
-
-        prepare_x0(0)
-        prepare_x0(1)
         project(0)
         neighbours(0)
         for i in range(n_units + LAG):
-            turn_next = i < n_units and units[i][0] == 0 and units[i][2] == SUBTILES - 1
-            if i < n_units:
-                pair_products(i)
-            if 1 <= i <= n_units:
-                shares(i - 1)
-            if i + 2 < SUBTILES:
-                prepare_x0(i + 2)
             if i + 1 < n_units:
                 project(i + 1)
                 neighbours(i + 1)
-            if turn_next:
-                turn_x(1, units[i][1], nc.scalar.copy)
+            if i < n_units:
+                pair_products(i)
             if i >= LAG:
                 split_by_sign(i - LAG)
-            if turn_next:
-                quantise_x(1, units[i][1])
             if i < n_units:
                 sums(i)
+                shares(i)
+            if i == SUBTILES:
+                for j in range(SUBTILES):
+                    turn_x(1, j)
+                    quantise_x(1, j)

@@ -184,8 +184,12 @@ def tile_dpfpattention_pa_kernel(tc, x, w_qk_words, w_qk_scales, out_0, out_1):
             rows = outs[n // 2][b, first_head : first_head + RANGE_HEADS].rearrange(
                 "h (p j) f -> p h j f", j=SUBTILES
             )
-            if i >= n_units - SUBTILES:
-                nc.sync.dma_start(out=rows[:, :, j, :], in_=result[:, :, j, :])
+            if i >= n_units - 2 * SUBTILES:
+                if j % 2 == 1:
+                    nc.sync.dma_start(
+                        out=rows[:, :, j - 1 : j + 1, :].rearrange("p h j f -> p h (j f)"),
+                        in_=result[:, :, j - 1 : j + 1, :].rearrange("p h j f -> p h (j f)"),
+                    )
             elif j == SUBTILES - 1:
                 nc.sync.dma_start(
                     out=rows.rearrange("p h j f -> p h (j f)"),

@@ -27,6 +27,10 @@ PAD = 4
 SCALE_ROWS = P * PACK // 32
 LAG = 2
 
+TALL_COLS = 128
+TALL_HEADS = TALL_COLS // D_HEAD
+TALL_UNITS = 4
+
 FLOPS = 2 * BATCH * TOKENS * D_MODEL * COLS
 
 
@@ -103,10 +107,26 @@ def tile_dpfpattention_pa_kernel(tc, x, w_qk_words, w_qk_scales, out_0, out_1):
 
         units = [(b, n, j) for b in range(BATCH) for n in range(RANGES) for j in range(SUBTILES)]
         n_units = len(units)
+        first_tall = n_units - TALL_UNITS
 
         def project(i):
             b, n, j = units[i]
             u = psum_u.tile([P, BANK_COLS], F32)
+            live["u", i] = u
+            if i >= first_tall:
+                first_col = BANK_COLS * n + TALL_COLS * j
+                for s in range(SUBTILES):
+                    for g in range(PASSES):
+                        nc.tensor.matmul_mx(
+                            out=u[:, TALL_COLS * s : TALL_COLS * (s + 1)],
+                            lhsT=x_codes[:, SUBTILES * b + s, P * g : P * (g + 1)].bitcast(FP8X4),
+                            lhsT_scale=x_scales[:, SUBTILES * b + s, P * g : P * (g + 1)],
+                            rhs=w_words[:, g, 2 * first_col : 2 * (first_col + TALL_COLS)].bitcast(FP4X4),
+                            rhs_scale=w_scales[:, g, first_col : first_col + TALL_COLS],
+                            start=(g == 0),
+                            stop=(g == PASSES - 1),
+                        )
+                return
             for g in range(PASSES):
                 nc.tensor.matmul_mx(
                     out=u[:],
@@ -166,6 +186,26 @@ def tile_dpfpattention_pa_kernel(tc, x, w_qk_words, w_qk_scales, out_0, out_1):
 
         def split_by_sign(i):
             b, n, j = units[i]
+            if i >= first_tall:
+                result = results.tile([P, TALL_HEADS, SUBTILES, 2 * D_HEAD], F32)
+                u_blocks = live["u", i][:].rearrange("p (s h c) -> p h s c", h=TALL_HEADS, c=D_HEAD)
+                share_blocks = live["share", i][:].rearrange("p (s h) c -> p h s c", h=TALL_HEADS)
+                for h in range(TALL_HEADS):
+                    for half, sign_test in enumerate((ALU.is_gt, ALU.is_lt)):
+                        nc.vector.scalar_tensor_tensor(
+                            out=result[:, h, :, D_HEAD * half : D_HEAD * (half + 1)],
+                            in0=u_blocks[:, h],
+                            scalar=0.0,
+                            in1=share_blocks[:, h],
+                            op0=sign_test,
+                            op1=ALU.mult,
+                        )
+                head = RANGE_HEADS * (n % 2) + TALL_HEADS * j
+                nc.sync.dma_start(
+                    out=outs[n // 2][b, head : head + TALL_HEADS].rearrange("h (p s) f -> p h (s f)", s=SUBTILES),
+                    in_=result[:].rearrange("p h s f -> p h (s f)"),
+                )
+                return
             if j == 0:
                 result = results.tile([P, RANGE_HEADS, SUBTILES, 2 * D_HEAD], F32)
                 live["result", b, n] = result

@@ -141,20 +141,21 @@ def tile_dpfpattention_pa_kernel(tc, x, w_qk_words, w_qk_scales, out_0, out_1):
 
         def neighbours(i):
             u = live["u", i]
-            shifted = work.tile([P, PAD + BANK_COLS], F32)
-            nc.scalar.copy(out=shifted[:, PAD:], in_=u[:])
-            before = shifted[:, PAD - 1 : PAD - 1 + BANK_COLS]
+            u_heads = u[:].rearrange("p (h c) -> p h c", c=D_HEAD)
+            shifted = work.tile([P, RANGE_HEADS, PAD + D_HEAD], F32)
+            nc.scalar.copy(out=shifted[:, :, PAD:], in_=u_heads)
             nc.scalar.mul(
-                out=before[:, 0:BANK_COLS:D_HEAD],
-                in_=u[:, D_HEAD - 1 : BANK_COLS : D_HEAD],
-                mul=-1.0,
+                out=shifted[:, :, PAD - 1 : PAD], in_=u_heads[:, :, D_HEAD - 1 : D_HEAD], mul=-1.0
             )
-            live["before", i] = before
+            live["before", i] = shifted[:, :, PAD - 1 : PAD - 1 + D_HEAD]
 
         def pair_products(i):
             pair = work.tile([P, BANK_COLS], F32)
             nc.vector.tensor_tensor(
-                out=pair[:], in0=live["u", i][:], in1=live["before", i], op=ALU.mult
+                out=pair[:].rearrange("p (h c) -> p h c", c=D_HEAD),
+                in0=live["u", i][:].rearrange("p (h c) -> p h c", c=D_HEAD),
+                in1=live["before", i],
+                op=ALU.mult,
             )
             live["pair", i] = pair
 

from contextlib import ExitStack

import concourse.mybir as mybir
from concourse.masks import make_identity

F32 = mybir.dt.float32
BF16 = mybir.dt.bfloat16
I32 = mybir.dt.int32
U32 = mybir.dt.uint32
U8 = mybir.dt.uint8
FP8X4 = mybir.dt.float8_e4m3fn_x4
FP4X4 = mybir.dt.float4_e2m1fn_x4
ALU = mybir.AluOpType
ACT = mybir.ActivationFunctionType

P = 128
PACK = 4
BATCH, TOKENS, D_MODEL = 2, 512, 1024
HEADS, D_HEAD = 16, 64
COLS = 2 * HEADS * D_HEAD
PASSES = D_MODEL // (P * PACK)
SUBTILES = TOKENS // P
BANK_COLS = 512
RANGES = COLS // BANK_COLS
RANGE_HEADS = BANK_COLS // D_HEAD
PAD = 4
SCALE_ROWS = P * PACK // 32
LAG = 2

TALL_COLS = 128
TALL_HEADS = TALL_COLS // D_HEAD
TALL_UNITS = 4

FLOPS = 2 * BATCH * TOKENS * D_MODEL * COLS


def tile_dpfpattention_pa_kernel(tc, x, w_qk_words, w_qk_scales, out_0, out_1):
    nc = tc.nc
    outs = (out_0, out_1)
    with ExitStack() as ctx:
        keep = ctx.enter_context(tc.tile_pool(name="keep", bufs=1))
        stage = ctx.enter_context(tc.tile_pool(name="stage", bufs=2))
        work = ctx.enter_context(tc.tile_pool(name="work", bufs=4))
        results = ctx.enter_context(tc.tile_pool(name="results", bufs=3))
        psum_x = ctx.enter_context(tc.psum_pool(name="psum_x", bufs=2))
        psum_u = ctx.enter_context(tc.psum_pool(name="psum_u", bufs=6))

        identity = keep.tile([P, P], F32)
        make_identity(nc, identity[:])

        x_sb = keep.tile([P, BATCH, SUBTILES, D_MODEL], BF16)
        w_words = keep.tile([P, PASSES, 2 * COLS], U8, align_bytes=64)
        w_scales = keep.tile([P, PASSES, COLS], U8, align_bytes=64)
        x_codes = keep.tile([P, BATCH * SUBTILES, PASSES * P], U32, align_bytes=64)
        x_scales = keep.tile([P, BATCH * SUBTILES, PASSES * P], U8, align_bytes=64)

        nc.vector.memset(w_scales[:].bitcast(I32), 0)
        x_rows = x.rearrange("b (p j) k -> b p j k", j=SUBTILES)
        words_i32 = w_qk_words.bitcast(I32).rearrange("g p c -> p g c")
        scales_i32 = w_qk_scales.bitcast(I32).rearrange("g q c -> q g c")
        plane_i32 = w_scales[:].bitcast(I32)

        def load_x(b, j):
            nc.sync.dma_start(out=x_sb[:, b, j, :], in_=x_rows[b, :, j, :])

        def load_w(n):
            nc.sync.dma_start(
                out=w_words[:, :, 2 * BANK_COLS * n : 2 * BANK_COLS * (n + 1)].bitcast(I32),
                in_=words_i32[:, :, BANK_COLS // 2 * n : BANK_COLS // 2 * (n + 1)],
            )

        load_x(0, 0)
        for r in range(4):
            nc.sync.dma_start(out=plane_i32[r:P:32, :, :], in_=scales_i32[r:SCALE_ROWS:4, :, :])
        load_w(0)
        for j in range(1, SUBTILES):
            load_x(0, j)
        for n in range(1, RANGES):
            load_w(n)
        nc.sync.dma_start(out=x_sb[:, 1, :, :], in_=x_rows[1])

        live = {}

        def turn_x(b, j):
            x_pairs = x_sb[:, b, j, :].bitcast(F32)
            turned = psum_x.tile([P, PASSES, 2, P], F32)
            for g in range(PASSES):
                for e in range(2):
                    nc.tensor.transpose(
                        turned[:, g, e, :],
                        x_pairs[:, 2 * P * g + e : 2 * P * (g + 1) : 2],
                        identity[:],
                    )
            grouped = stage.tile([P, PASSES * P * PACK], BF16, align_bytes=64)
            nc.scalar.copy(
                out=grouped[:].bitcast(F32).rearrange("p (g r e) -> p g r e", g=PASSES, e=2),
                in_=turned[:].rearrange("p g e r -> p g r e"),
            )
            live["grouped", b, j] = grouped

        def quantise_x(b, j):
            nc.vector.quantize_mx(
                out=x_codes[:, SUBTILES * b + j, :].bitcast(FP8X4),
                scales=x_scales[:, SUBTILES * b + j, :],
                in_=live["grouped", b, j][:],
            )

        units = [(b, n, j) for b in range(BATCH) for n in range(RANGES) for j in range(SUBTILES)]
        n_units = len(units)
        first_tall = n_units - TALL_UNITS

        def project(i):
            b, n, j = units[i]
            u = psum_u.tile([P, BANK_COLS], F32)
            live["u", i] = u
            if i >= first_tall:
                first_col = BANK_COLS * n + TALL_COLS * j
                for s in range(SUBTILES):
                    for g in range(PASSES):
                        nc.tensor.matmul_mx(
                            out=u[:, TALL_COLS * s : TALL_COLS * (s + 1)],
                            lhsT=x_codes[:, SUBTILES * b + s, P * g : P * (g + 1)].bitcast(FP8X4),
                            lhsT_scale=x_scales[:, SUBTILES * b + s, P * g : P * (g + 1)],
                            rhs=w_words[:, g, 2 * first_col : 2 * (first_col + TALL_COLS)].bitcast(FP4X4),
                            rhs_scale=w_scales[:, g, first_col : first_col + TALL_COLS],
                            start=(g == 0),
                            stop=(g == PASSES - 1),
                        )
                return
            for g in range(PASSES):
                nc.tensor.matmul_mx(
                    out=u[:],
                    lhsT=x_codes[:, SUBTILES * b + j, P * g : P * (g + 1)].bitcast(FP8X4),
                    lhsT_scale=x_scales[:, SUBTILES * b + j, P * g : P * (g + 1)],
                    rhs=w_words[:, g, 2 * BANK_COLS * n : 2 * BANK_COLS * (n + 1)].bitcast(FP4X4),
                    rhs_scale=w_scales[:, g, BANK_COLS * n : BANK_COLS * (n + 1)],
                    start=(g == 0),
                    stop=(g == PASSES - 1),
                )
            live["u", i] = u

        def neighbours(i):
            u = live["u", i]
            u_heads = u[:].rearrange("p (h c) -> p h c", c=D_HEAD)
            shifted = work.tile([P, RANGE_HEADS, PAD + D_HEAD], F32)
            nc.scalar.copy(out=shifted[:, :, PAD:], in_=u_heads)
            nc.scalar.mul(
                out=shifted[:, :, PAD - 1 : PAD], in_=u_heads[:, :, D_HEAD - 1 : D_HEAD], mul=-1.0
            )
            live["before", i] = shifted[:, :, PAD - 1 : PAD - 1 + D_HEAD]

        def pair_products(i):
            pair = work.tile([P, BANK_COLS], F32)
            nc.vector.tensor_tensor(
                out=pair[:].rearrange("p (h c) -> p h c", c=D_HEAD),
                in0=live["u", i][:].rearrange("p (h c) -> p h c", c=D_HEAD),
                in1=live["before", i],
                op=ALU.mult,
            )
            live["pair", i] = pair

        def sums(i):
            pair = live["pair", i]
            kept = work.tile([P, RANGE_HEADS, D_HEAD], F32)
            total = work.tile([P, RANGE_HEADS], F32)
            for h in range(RANGE_HEADS):
                nc.scalar.activation(
                    out=kept[:, h, :],
                    in_=pair[:, D_HEAD * h : D_HEAD * (h + 1)],
                    func=ACT.Relu,
                    accum_out=total[:, h : h + 1],
                )
            live["kept", i] = kept
            live["total", i] = total

        def shares(i):
            inverse = work.tile([P, RANGE_HEADS], F32)
            nc.vector.reciprocal(out=inverse[:], in_=live["total", i][:])
            share = work.tile([P, RANGE_HEADS, D_HEAD], F32)
            nc.gpsimd.tensor_tensor(
                out=share[:],
                in0=live["kept", i][:],
                in1=inverse[:].unsqueeze(2).to_broadcast([P, RANGE_HEADS, D_HEAD]),
                op=ALU.mult,
            )
            live["share", i] = share

        def split_by_sign(i):
            b, n, j = units[i]
            if i >= first_tall:
                result = results.tile([P, TALL_HEADS, SUBTILES, 2 * D_HEAD], F32)
                u_blocks = live["u", i][:].rearrange("p (s h c) -> p h s c", h=TALL_HEADS, c=D_HEAD)
                share_blocks = live["share", i][:].rearrange("p (s h) c -> p h s c", h=TALL_HEADS)
                for h in range(TALL_HEADS):
                    for half, sign_test in enumerate((ALU.is_gt, ALU.is_lt)):
                        nc.vector.scalar_tensor_tensor(
                            out=result[:, h, :, D_HEAD * half : D_HEAD * (half + 1)],
                            in0=u_blocks[:, h],
                            scalar=0.0,
                            in1=share_blocks[:, h],
                            op0=sign_test,
                            op1=ALU.mult,
                        )
                head = RANGE_HEADS * (n % 2) + TALL_HEADS * j
                nc.sync.dma_start(
                    out=outs[n // 2][b, head : head + TALL_HEADS].rearrange("h (p s) f -> p h (s f)", s=SUBTILES),
                    in_=result[:].rearrange("p h s f -> p h (s f)"),
                )
                return
            if j == 0:
                result = results.tile([P, RANGE_HEADS, SUBTILES, 2 * D_HEAD], F32)
                live["result", b, n] = result
            result = live["result", b, n]
            u_heads = live["u", i][:].rearrange("p (h c) -> p h c", c=D_HEAD)
            for half, sign_test in enumerate((ALU.is_gt, ALU.is_lt)):
                nc.vector.scalar_tensor_tensor(
                    out=result[:, :, j, D_HEAD * half : D_HEAD * (half + 1)],
                    in0=u_heads,
                    scalar=0.0,
                    in1=live["share", i][:],
                    op0=sign_test,
                    op1=ALU.mult,
                )
            first_head = RANGE_HEADS * (n % 2)
            rows = outs[n // 2][b, first_head : first_head + RANGE_HEADS].rearrange(
                "h (p j) f -> p h j f", j=SUBTILES
            )
            if i >= n_units - 2 * SUBTILES:
                if j % 2 == 1:
                    nc.sync.dma_start(
                        out=rows[:, :, j - 1 : j + 1, :].rearrange("p h j f -> p h (j f)"),
                        in_=result[:, :, j - 1 : j + 1, :].rearrange("p h j f -> p h (j f)"),
                    )
            elif j == SUBTILES - 1:
                nc.sync.dma_start(
                    out=rows.rearrange("p h j f -> p h (j f)"),
                    in_=result[:].rearrange("p h j f -> p h (j f)"),
                )

        for j in range(SUBTILES):
            turn_x(0, j)
            quantise_x(0, j)
        project(0)
        neighbours(0)
        for i in range(n_units + LAG):
            if i + 1 < n_units:
                project(i + 1)
                neighbours(i + 1)
            if i < n_units:
                pair_products(i)
            if i >= LAG:
                split_by_sign(i - LAG)
            if i < n_units:
                sums(i)
                shares(i)
            if i == SUBTILES:
                for j in range(SUBTILES):
                    turn_x(1, j)
                    quantise_x(1, j)
